import numpy as np
import ml_dtypes


def mxq(x, axis, fmt="e4m3"):
    dtype, down = {"e4m3": (ml_dtypes.float8_e4m3fn, 7), "e5m2": (ml_dtypes.float8_e5m2, 14)}[fmt]
    v = np.moveaxis(np.asarray(x, np.float32).astype(ml_dtypes.bfloat16).astype(np.float64), axis, -1)
    blocks = v.reshape(v.shape[:-1] + (-1, 32))
    amax = np.abs(blocks).max(-1, keepdims=True)
    byte = np.maximum(np.where(amax > 0, np.frexp(amax)[1] - 1 + 127, 0) - down, 1)
    scale = np.exp2(byte - 127.0)
    codes = (blocks / scale).astype(np.float32).astype(dtype).astype(np.float64)
    return np.moveaxis((codes * scale).reshape(v.shape), -1, axis)


WIDE = False


def mx_kscale(k):
    if not WIDE:
        return np.ones(k)
    levels = np.array([10, -10, 5, -5, 0])
    if k % 512:
        return np.exp2(np.random.permutation(np.resize(levels, k // 32))).repeat(32)
    a = np.empty((k // 512, 16))
    for p in range(k // 512):
        a[p, :8] = np.random.permutation(np.resize(levels, 8))
        for g in range(8):
            far = levels[np.abs(levels - a[p, g]) >= 10]
            a[p, g + 8] = far[np.random.randint(len(far))]
    return np.exp2(a.ravel()).repeat(32)


BF16 = ml_dtypes.bfloat16


def bf(x):
    return np.asarray(x, np.float32).astype(BF16)


def f64(x):
    return np.asarray(x).astype(np.float64)


N, H, S, R, T = 4096, 512, 4, 128, 128


def sigmoid(v):
    return 1.0 / (1.0 + np.exp(-v))


def setup_inputs():
    s, t = mx_kscale(H), mx_kscale(H)
    g = np.exp(np.random.standard_normal((S, N)))
    return {"encodings": bf(np.random.standard_normal((N, H)) * s),
            "alphas": bf(g / g.sum(axis=0, keepdims=True)),
            "W1": bf(np.random.standard_normal((S, H, H)) * 1.4 / np.sqrt(H) / s[None, :, None] * t[None, None, :]),
            "b1": bf(np.random.standard_normal((S, H)) * 0.3 * t[None, :]),
            "W2": bf(np.random.standard_normal((S, H, T)) * 2.0 / np.sqrt(H) / t[None, :, None]),
            "b2": bf(np.random.standard_normal((S, T)) * 0.5)}


def reference(encodings, alphas, W1, b1, W2, b2):
    h0 = np.maximum(f64(encodings), 0.0)
    h1 = np.maximum((mxq(h0, 1, "e4m3") @ mxq(f64(W1), 1, "e4m3")) + f64(b1)[:, None, :], 0.0)
    out = sigmoid((mxq(h1, 2, "e4m3") @ mxq(f64(W2), 1, "e4m3")) + f64(b2)[:, None, :])
    return np.sum(f64(alphas)[:, :, None] * out, axis=0)

@@ -1,0 +1,357 @@
+from contextlib import ExitStack
+
+import concourse.mybir as mybir
+from concourse.masks import make_identity
+
+N_TOK, H, S, T = 4096, 512, 4, 128
+FLOPS = 2 * N_TOK * H * H * S + 2 * N_TOK * H * T * S
+
+F32 = mybir.dt.float32
+BF16 = mybir.dt.bfloat16
+U32 = mybir.dt.uint32
+U8 = mybir.dt.uint8
+FP8X4 = mybir.dt.float8_e4m3fn_x4
+BANK1 = F32
+
+RELU = mybir.ActivationFunctionType.Relu
+SIGMOID = mybir.ActivationFunctionType.Sigmoid
+ADD = mybir.AluOpType.add
+MULT = mybir.AluOpType.mult
+MAX = mybir.AluOpType.max
+
+P = 128
+PACK = 4
+GT = 512
+NG = N_TOK // GT
+NU = NG * S
+TAIL_SPLIT = 2
+ITEMS = [(u, 0, GT) for u in range(NU - 1)] + [
+    (NU - 1, h * (GT // TAIL_SPLIT), GT // TAIL_SPLIT) for h in range(TAIL_SPLIT)
+]
+NI = len(ITEMS)
+
+
+def tile_moe_pb_kernel(tc, encodings, alphas, W1, b1, W2, b2, out):
+    nc = tc.nc
+
+    with ExitStack() as ctx:
+        keep = ctx.enter_context(tc.tile_pool(name="keep", bufs=1))
+        ring2 = ctx.enter_context(tc.tile_pool(name="ring2", bufs=2))
+        ring3 = ctx.enter_context(tc.tile_pool(name="ring3", bufs=3))
+        ring4 = ctx.enter_context(tc.tile_pool(name="ring4", bufs=4))
+        psum = ctx.enter_context(tc.psum_pool(name="psum", bufs=8))
+        ctx.enter_context(tc.manual_schedule())
+
+        enc = {}
+        w1_raw = {}
+        w1_grouped = {}
+        w1_codes = {}
+        w1_scales = {}
+        h0_relu = {}
+        h0_turned = {}
+        h0_grouped = {}
+        h0_codes = {}
+        h0_scales = {}
+        bank1 = {}
+        h1_rows = {}
+        h1_grouped = {}
+        h1_codes = {}
+        h1_scales = {}
+        bank2 = {}
+        prob = {}
+        prob_turned = {}
+        mixed = {}
+
+        def load_enc(g, b):
+            enc[(g, b)] = keep.tile([P, 2, H], BF16, name="enc%d_%d" % (g, b), tag="enc%d_%d" % (g, b))
+            r0 = g * GT + b * 2 * P
+            nc.sync.dma_start(
+                out=enc[(g, b)][:], in_=encodings[r0 : r0 + 2 * P, :].rearrange("(j p) k -> p j k", p=P)
+            )
+
+        def load_w1(s):
+            w1_raw[s] = keep.tile([P, PACK, H], BF16, name="w1raw%d" % s, tag="w1raw%d" % s)
+            nc.sync.dma_start(out=w1_raw[s][:], in_=W1[s].rearrange("(p j) c -> p j c", j=PACK))
+
+        ident = keep.tile([P, P], F32, name="ident", tag="ident")
+        make_identity(nc, ident[:])
+
+        b1_bf = keep.tile([P, S, PACK], BF16, name="b1_bf", tag="b1_bf")
+        nc.scalar.dma_start(out=b1_bf[:], in_=b1.rearrange("s (p t) -> p s t", t=PACK))
+        b2_bf = keep.tile([P, S], BF16, name="b2_bf", tag="b2_bf")
+        with nc.allow_non_contiguous_dma(reason="512 bias values, one to a partition, once"):
+            nc.scalar.dma_start(out=b2_bf[:], in_=b2.rearrange("s t -> t s"))
+
+        load_enc(0, 0)
+        load_enc(0, 1)
+        load_w1(0)
+        load_w1(1)
+        load_enc(1, 0)
+        load_enc(1, 1)
+        load_w1(2)
+        w2_raw = keep.tile([P, S, PACK, T], BF16, name="w2_raw", tag="w2_raw")
+        nc.sync.dma_start(out=w2_raw[:], in_=W2.rearrange("s (p j) c -> p s j c", j=PACK))
+        load_w1(3)
+        al_raw = keep.tile([P, P], BF16, name="al_raw", tag="al_raw")
+        nc.sync.dma_start(out=al_raw[:], in_=alphas.rearrange("s (j p) -> (s j) p", p=P))
+        for g in range(2, NG):
+            load_enc(g, 0)
+            load_enc(g, 1)
+
+        def relu_enc(g, b):
+            h0_relu[(g, b)] = ring4.tile([P, 2, H], BF16, name="h0_relu", tag="h0_relu")
+            nc.vector.tensor_scalar(
+                out=h0_relu[(g, b)][:].rearrange("p j k -> p (j k)"),
+                in0=enc[(g, b)][:].rearrange("p j k -> p (j k)"),
+                scalar1=0.0,
+                scalar2=None,
+                op0=MAX,
+            )
+
+        def turn_enc(g, b):
+            xt = psum.tile([P, 2, 2, P], F32, name="xt", tag="bank")
+            h0_turned[(g, b)] = xt
+            for jj in range(2):
+                words = h0_relu[(g, b)][:, jj, :].bitcast(F32)
+                for u in range(2):
+                    nc.tensor.transpose(xt[:, jj, u, :], words[:, u : H // 2 : 2], ident[:])
+
+        def copy_enc(g, b, engine):
+            if b == 0:
+                h0_grouped[g] = ring2.tile([P, GT * PACK], BF16, name="h0_grouped", tag="h0_grouped", align_bytes=64)
+            dst = h0_grouped[g][:, b * 1024 : (b + 1) * 1024].bitcast(F32).rearrange(
+                "p (jj r u) -> p jj r u", jj=2, u=2
+            )
+            src = h0_turned[(g, b)][:].rearrange("p jj u r -> p jj r u")
+            if engine == "scalar":
+                nc.scalar.copy(out=dst, in_=src)
+            else:
+                nc.vector.tensor_copy(out=dst, in_=src)
+
+        def quantize_enc(g):
+            h0_codes[g] = ring2.tile([P, GT], U32, name="h0_codes", tag="h0_codes", align_bytes=64)
+            h0_scales[g] = ring2.tile([P, GT], U8, name="h0_scales", tag="h0_scales", align_bytes=64)
+            nc.vector.quantize_mx(out=h0_codes[g][:].bitcast(FP8X4), scales=h0_scales[g][:], in_=h0_grouped[g][:])
+
+        def group_w1(s, t0, nt, engine):
+            if t0 == 0:
+                w1_grouped[s] = ring2.tile([P, H * PACK], BF16, name="w1_grouped", tag="w1_grouped", align_bytes=64)
+            dst = w1_grouped[s][:, t0 * H : (t0 + nt) * H].rearrange("p (t m j) -> p t m j", t=nt, j=PACK)
+            src = w1_raw[s][:].rearrange("p j (m t) -> p t m j", t=PACK)[:, t0 : t0 + nt]
+            if engine == "scalar":
+                nc.scalar.copy(out=dst, in_=src)
+            else:
+                nc.vector.tensor_copy(out=dst, in_=src)
+
+        def quantize_w1(s, t0, nt):
+            if t0 == 0:
+                w1_codes[s] = keep.tile([P, H], U32, name="w1c%d" % s, tag="w1c%d" % s, align_bytes=64)
+                w1_scales[s] = keep.tile([P, H], U8, name="w1s%d" % s, tag="w1s%d" % s, align_bytes=64)
+            nc.vector.quantize_mx(
+                out=w1_codes[s][:, t0 * P : (t0 + nt) * P].bitcast(FP8X4),
+                scales=w1_scales[s][:, t0 * P : (t0 + nt) * P],
+                in_=w1_grouped[s][:, t0 * H : (t0 + nt) * H],
+            )
+
+        def stage1(u):
+            g, s = divmod(u, S)
+            for t in range(PACK):
+                bank = psum.tile([P, GT], BANK1, name="bank1", tag="bank")
+                bank1[(u, t)] = bank
+                cols = slice(t * P, (t + 1) * P)
+                nc.tensor.matmul_mx(
+                    out=bank[:],
+                    lhsT=w1_codes[s][:, cols].bitcast(FP8X4),
+                    lhsT_scale=w1_scales[s][:, cols],
+                    rhs=h0_codes[g][:].bitcast(FP8X4),
+                    rhs_scale=h0_scales[g][:],
+                    start=True,
+                    stop=True,
+                )
+
+        V_READS = {}
+
+        def read1_alloc(k):
+            n = ITEMS[k][2]
+            h1_rows[k] = ring3.tile([P, PACK, n], BF16, name="h1_rows", tag="h1_rows")
+
+        def read1(k, t, engine):
+            u, n0, n = ITEMS[k]
+            s = u % S
+            bias = b1_f[:, s * PACK + t : s * PACK + t + 1]
+            if engine == "scalar":
+                nc.scalar.activation(
+                    out=h1_rows[k][:, t, :], in_=bank1[(u, t)][:, n0 : n0 + n], func=RELU, bias=bias, scale=1.0
+                )
+            else:
+                nc.vector.tensor_scalar(
+                    out=h1_rows[k][:, t, :],
+                    in0=bank1[(u, t)][:, n0 : n0 + n],
+                    scalar1=bias,
+                    scalar2=0.0,
+                    op0=ADD,
+                    op1=MAX,
+                )
+
+        def group_h1(k):
+            n = ITEMS[k][2]
+            h1_grouped[k] = ring2.tile([P, n * PACK], BF16, name="h1_grouped", tag="h1_grouped", align_bytes=64)
+            nc.vector.tensor_copy(
+                out=h1_grouped[k][:].rearrange("p (c i t) -> p c t i", i=4, t=PACK),
+                in_=h1_rows[k][:].rearrange("p t (c i) -> p c t i", i=4),
+            )
+
+        def quantize_h1(k):
+            n = ITEMS[k][2]
+            h1_codes[k] = ring3.tile([P, n], U32, name="h1_codes", tag="h1_codes", align_bytes=64)
+            h1_scales[k] = ring3.tile([P, n], U8, name="h1_scales", tag="h1_scales", align_bytes=64)
+            nc.vector.quantize_mx(out=h1_codes[k][:].bitcast(FP8X4), scales=h1_scales[k][:], in_=h1_grouped[k][:])
+
+        def stage2(k):
+            u, n0, n = ITEMS[k]
+            s = u % S
+            bank2[k] = psum.tile([P, n], F32, name="bank2", tag="bank")
+            cols = slice(s * T, (s + 1) * T)
+            nc.tensor.matmul_mx(
+                out=bank2[k][:],
+                lhsT=w2_codes[:, cols].bitcast(FP8X4),
+                lhsT_scale=w2_scales[:, cols],
+                rhs=h1_codes[k][:].bitcast(FP8X4),
+                rhs_scale=h1_scales[k][:],
+                start=True,
+                stop=True,
+            )
+
+        def sigmoid2(k):
+            u, n0, n = ITEMS[k]
+            s = u % S
+            prob[k] = ring3.tile([P, n], F32, name="prob", tag="prob")
+            nc.scalar.activation(out=prob[k][:], in_=bank2[k][:], func=SIGMOID, bias=b2_f[:, s : s + 1], scale=1.0)
+
+        def turn_prob(k):
+            n = ITEMS[k][2]
+            prob_turned[k] = psum.tile([P, n // P, T], F32, name="prob_turned", tag="bank")
+            for j in range(n // P):
+                nc.tensor.transpose(prob_turned[k][:, j, :], prob[k][:, j * P : (j + 1) * P], ident[:])
+
+        def mix(k):
+            u, n0, n = ITEMS[k]
+            g, s = divmod(u, S)
+            if s == 0:
+                mixed[g] = ring2.tile([P, 4, T], F32, name="mixed", tag="mixed")
+            for jj in range(n // P):
+                j = n0 // P + jj
+                col = s * (N_TOK // P) + g * 4 + j
+                if s == 0:
+                    nc.vector.tensor_scalar(
+                        out=mixed[g][:, j, :],
+                        in0=prob_turned[k][:, jj, :],
+                        scalar1=al_f[:, col : col + 1],
+                        scalar2=None,
+                        op0=MULT,
+                    )
+                else:
+                    nc.vector.scalar_tensor_tensor(
+                        out=mixed[g][:, j, :],
+                        in0=prob_turned[k][:, jj, :],
+                        scalar=al_f[:, col : col + 1],
+                        in1=mixed[g][:, j, :],
+                        op0=MULT,
+                        op1=ADD,
+                    )
+
+        def store(k):
+            u, n0, n = ITEMS[k]
+            g = u // S
+            r0 = g * GT + n0
+            nc.sync.dma_start(
+                out=out[r0 : r0 + n, :].rearrange("(j p) t -> p j t", p=P),
+                in_=mixed[g][:, n0 // P : (n0 + n) // P, :],
+            )
+
+        warm_in = keep.tile([P, 1], F32, name="warm_in", tag="warm_in")
+        warm_out = keep.tile([P, 1], F32, name="warm_out", tag="warm_out")
+        nc.vector.memset(warm_in[:], 0.0)
+        nc.scalar.activation(out=warm_out[:], in_=warm_in[:], func=SIGMOID)
+
+        b1_f = keep.tile([P, S * PACK], F32, name="b1_f", tag="b1_f")
+        b2_f = keep.tile([P, S], F32, name="b2_f", tag="b2_f")
+        al_cast = keep.tile([P, P], F32, name="al_cast", tag="al_cast")
+        al_f = keep.tile([P, P], F32, name="al_f", tag="al_f")
+        w2_grouped = keep.tile([P, S * T * PACK], BF16, name="w2_grouped", tag="w2_grouped", align_bytes=64)
+        w2_codes = keep.tile([P, S * T], U32, name="w2_codes", tag="w2_codes", align_bytes=64)
+        w2_scales = keep.tile([P, S * T], U8, name="w2_scales", tag="w2_scales", align_bytes=64)
+
+        relu_enc(0, 0)
+        turn_enc(0, 0)
+        copy_enc(0, 0, "scalar")
+        relu_enc(0, 1)
+        turn_enc(0, 1)
+        copy_enc(0, 1, "vector")
+        group_w1(0, 0, 2, "vector")
+        group_w1(0, 2, 2, "scalar")
+        nc.vector.tensor_copy(out=b1_f[:], in_=b1_bf[:].rearrange("p s t -> p (s t)"))
+        quantize_enc(0)
+        quantize_w1(0, 0, 2)
+        group_w1(1, 0, 4, "vector")
+        quantize_w1(0, 2, 2)
+        relu_enc(1, 0)
+
+        for i in range(-1, NI + 4):
+            if 0 <= i - 2 < NI:
+                stage2(i - 2)
+            if 0 <= i - 3 < NI:
+                turn_prob(i - 3)
+            if i == 1:
+                al_turned = psum.tile([P, P], F32, name="al_turned", tag="bank")
+                nc.tensor.transpose(al_turned[:], al_cast[:], ident[:])
+            if (i + 4) % 4 == 0 and 1 <= (i + 4) // 4 < NG:
+                turn_enc((i + 4) // 4, 0)
+            if (i + 3) % 4 == 0 and 1 <= (i + 3) // 4 < NG:
+                turn_enc((i + 3) // 4, 1)
+            if 0 <= i + 1 < NU:
+                stage1(i + 1)
+            if 0 <= i < NI:
+                read1_alloc(i)
+                for t in range(PACK):
+                    if t not in V_READS.get(str(i), []):
+                        read1(i, t, "scalar")
+            if 0 <= i - 2 < NI:
+                sigmoid2(i - 2)
+            if (i + 4) % 4 == 0 and 1 <= (i + 4) // 4 < NG:
+                copy_enc((i + 4) // 4, 0, "scalar")
+            if 0 <= i < NI:
+                for t in V_READS.get(str(i), []):
+                    read1(i, t, "vector")
+            if 0 <= i - 1 < NI:
+                group_h1(i - 1)
+            if (i + 5) % 4 == 0 and 2 <= (i + 5) // 4 < NG:
+                relu_enc((i + 5) // 4, 0)
+            if (i + 4) % 4 == 0 and 1 <= (i + 4) // 4 < NG:
+                relu_enc((i + 4) // 4, 1)
+            if i == -1:
+                quantize_w1(1, 0, 4)
+                group_w1(2, 0, 4, "vector")
+                nc.vector.tensor_copy(
+                    out=w2_grouped[:].rearrange("p (s c j) -> p s c j", s=S, j=PACK),
+                    in_=w2_raw[:].rearrange("p s j c -> p s c j"),
+                )
+                quantize_w1(2, 0, 4)
+            if i == 0:
+                group_w1(3, 0, 4, "vector")
+                nc.vector.quantize_mx(out=w2_codes[:].bitcast(FP8X4), scales=w2_scales[:], in_=w2_grouped[:])
+                nc.vector.tensor_copy(out=b2_f[:], in_=b2_bf[:])
+                nc.vector.tensor_copy(out=al_cast[:], in_=al_raw[:])
+                quantize_w1(3, 0, 4)
+            if i == 1:
+                nc.vector.tensor_copy(out=al_f[:], in_=al_turned[:])
+            if 0 <= i - 3 < NI:
+                mix(i - 3)
+            if 0 <= i - 1 < NI:
+                quantize_h1(i - 1)
+            if (i + 3) % 4 == 0 and 1 <= (i + 3) // 4 < NG:
+                copy_enc((i + 3) // 4, 1, "vector")
+            if (i + 2) % 4 == 0 and 1 <= (i + 2) // 4 < NG:
+                quantize_enc((i + 2) // 4)
+            if 0 <= i - 3 < NI and ITEMS[i - 3][0] % S == S - 1:
+                store(i - 3)

@@ -197,8 +197,8 @@ def tile_moe_pb_kernel(tc, encodings, alphas, W1, b1, W2, b2, out):
             n = ITEMS[k][2]
             h1_grouped[k] = ring2.tile([P, n * PACK], BF16, name="h1_grouped", tag="h1_grouped", align_bytes=64)
             nc.vector.tensor_copy(
-                out=h1_grouped[k][:].rearrange("p (c i t) -> p c t i", i=4, t=PACK),
-                in_=h1_rows[k][:].rearrange("p t (c i) -> p c t i", i=4),
+                out=h1_grouped[k][:].rearrange("p (n t) -> p n t", t=PACK),
+                in_=h1_rows[k][:].rearrange("p t n -> p n t"),
             )
 
         def quantize_h1(k):

@@ -29,6 +29,7 @@ ITEMS = [(u, 0, GT) for u in range(NU - 1)] + [
     (NU - 1, h * (GT // TAIL_SPLIT), GT // TAIL_SPLIT) for h in range(TAIL_SPLIT)
 ]
 NI = len(ITEMS)
+LAST_GROUP_ALL_SCALAR = 3
 
 
 def tile_moe_pb_kernel(tc, encodings, alphas, W1, b1, W2, b2, out):
@@ -197,14 +198,14 @@ def tile_moe_pb_kernel(tc, encodings, alphas, W1, b1, W2, b2, out):
             n = ITEMS[k][2]
             h1_grouped[k] = ring2.tile([P, n * PACK], BF16, name="h1_grouped", tag="h1_grouped", align_bytes=64)
             nc.vector.tensor_copy(
-                out=h1_grouped[k][:].rearrange("p (n t) -> p n t", t=PACK),
-                in_=h1_rows[k][:].rearrange("p t n -> p n t"),
+                out=h1_grouped[k][:].rearrange("p (c i t) -> p c t i", i=4, t=PACK),
+                in_=h1_rows[k][:].rearrange("p t (c i) -> p c t i", i=4),
             )
 
         def quantize_h1(k):
             n = ITEMS[k][2]
-            h1_codes[k] = ring3.tile([P, n], U32, name="h1_codes", tag="h1_codes", align_bytes=64)
-            h1_scales[k] = ring3.tile([P, n], U8, name="h1_scales", tag="h1_scales", align_bytes=64)
+            h1_codes[k] = ring4.tile([P, n], U32, name="h1_codes", tag="h1_codes", align_bytes=64)
+            h1_scales[k] = ring4.tile([P, n], U8, name="h1_scales", tag="h1_scales", align_bytes=64)
             nc.vector.quantize_mx(out=h1_codes[k][:].bitcast(FP8X4), scales=h1_scales[k][:], in_=h1_grouped[k][:])
 
         def stage2(k):
@@ -293,15 +294,16 @@ def tile_moe_pb_kernel(tc, encodings, alphas, W1, b1, W2, b2, out):
         nc.vector.tensor_copy(out=b1_f[:], in_=b1_bf[:].rearrange("p s t -> p (s t)"))
         quantize_enc(0)
         quantize_w1(0, 0, 2)
-        group_w1(1, 0, 4, "vector")
         quantize_w1(0, 2, 2)
+        group_w1(1, 0, 2, "vector")
+        group_w1(1, 2, 2, "scalar")
         relu_enc(1, 0)
 
-        for i in range(-1, NI + 4):
-            if 0 <= i - 2 < NI:
-                stage2(i - 2)
+        for i in range(-1, NI + 5):
             if 0 <= i - 3 < NI:
-                turn_prob(i - 3)
+                stage2(i - 3)
+            if 0 <= i - 4 < NI:
+                turn_prob(i - 4)
             if i == 1:
                 al_turned = psum.tile([P, P], F32, name="al_turned", tag="bank")
                 nc.tensor.transpose(al_turned[:], al_cast[:], ident[:])
@@ -316,10 +318,12 @@ def tile_moe_pb_kernel(tc, encodings, alphas, W1, b1, W2, b2, out):
                 for t in range(PACK):
                     if t not in V_READS.get(str(i), []):
                         read1(i, t, "scalar")
-            if 0 <= i - 2 < NI:
-                sigmoid2(i - 2)
+            if 0 <= i - 3 < NI:
+                sigmoid2(i - 3)
             if (i + 4) % 4 == 0 and 1 <= (i + 4) // 4 < NG:
                 copy_enc((i + 4) // 4, 0, "scalar")
+            if (i + 3) % 4 == 0 and 1 <= (i + 3) // 4 <= LAST_GROUP_ALL_SCALAR:
+                copy_enc((i + 3) // 4, 1, "scalar")
             if 0 <= i < NI:
                 for t in V_READS.get(str(i), []):
                     read1(i, t, "vector")
@@ -345,13 +349,13 @@ def tile_moe_pb_kernel(tc, encodings, alphas, W1, b1, W2, b2, out):
                 quantize_w1(3, 0, 4)
             if i == 1:
                 nc.vector.tensor_copy(out=al_f[:], in_=al_turned[:])
-            if 0 <= i - 3 < NI:
-                mix(i - 3)
+            if 0 <= i - 4 < NI:
+                mix(i - 4)
             if 0 <= i - 1 < NI:
                 quantize_h1(i - 1)
-            if (i + 3) % 4 == 0 and 1 <= (i + 3) // 4 < NG:
+            if (i + 3) % 4 == 0 and LAST_GROUP_ALL_SCALAR < (i + 3) // 4 < NG:
                 copy_enc((i + 3) // 4, 1, "vector")
             if (i + 2) % 4 == 0 and 1 <= (i + 2) // 4 < NG:
                 quantize_enc((i + 2) // 4)
-            if 0 <= i - 3 < NI and ITEMS[i - 3][0] % S == S - 1:
-                store(i - 3)
+            if 0 <= i - 4 < NI and ITEMS[i - 4][0] % S == S - 1:
+                store(i - 4)

@@ -170,7 +170,11 @@ def tile_moe_pb_kernel(tc, encodings, alphas, W1, b1, W2, b2, out):
                     stop=True,
                 )
 
-        V_READS = {}
+        def vector_reads(k):
+            u, n0, n = ITEMS[k]
+            if u % S == S - 1 and u >= S and n0 == 0:
+                return [PACK - 1]
+            return []
 
         def read1_alloc(k):
             n = ITEMS[k][2]
@@ -316,7 +320,7 @@ def tile_moe_pb_kernel(tc, encodings, alphas, W1, b1, W2, b2, out):
             if 0 <= i < NI:
                 read1_alloc(i)
                 for t in range(PACK):
-                    if t not in V_READS.get(str(i), []):
+                    if t not in vector_reads(i):
                         read1(i, t, "scalar")
             if 0 <= i - 3 < NI:
                 sigmoid2(i - 3)
@@ -325,7 +329,7 @@ def tile_moe_pb_kernel(tc, encodings, alphas, W1, b1, W2, b2, out):
             if (i + 3) % 4 == 0 and 1 <= (i + 3) // 4 <= LAST_GROUP_ALL_SCALAR:
                 copy_enc((i + 3) // 4, 1, "scalar")
             if 0 <= i < NI:
-                for t in V_READS.get(str(i), []):
+                for t in vector_reads(i):
                     read1(i, t, "vector")
             if 0 <= i - 1 < NI:
                 group_h1(i - 1)

from contextlib import ExitStack

import concourse.mybir as mybir
from concourse.masks import make_identity

N_TOK, H, S, T = 4096, 512, 4, 128
FLOPS = 2 * N_TOK * H * H * S + 2 * N_TOK * H * T * S

F32 = mybir.dt.float32
BF16 = mybir.dt.bfloat16
U32 = mybir.dt.uint32
U8 = mybir.dt.uint8
FP8X4 = mybir.dt.float8_e4m3fn_x4
BANK1 = F32

RELU = mybir.ActivationFunctionType.Relu
SIGMOID = mybir.ActivationFunctionType.Sigmoid
ADD = mybir.AluOpType.add
MULT = mybir.AluOpType.mult
MAX = mybir.AluOpType.max

P = 128
PACK = 4
GT = 512
NG = N_TOK // GT
NU = NG * S
TAIL_SPLIT = 2
ITEMS = [(u, 0, GT) for u in range(NU - 1)] + [
    (NU - 1, h * (GT // TAIL_SPLIT), GT // TAIL_SPLIT) for h in range(TAIL_SPLIT)
]
NI = len(ITEMS)
LAST_GROUP_ALL_SCALAR = 3


def tile_moe_pb_kernel(tc, encodings, alphas, W1, b1, W2, b2, out):
    nc = tc.nc

    with ExitStack() as ctx:
        keep = ctx.enter_context(tc.tile_pool(name="keep", bufs=1))
        ring2 = ctx.enter_context(tc.tile_pool(name="ring2", bufs=2))
        ring3 = ctx.enter_context(tc.tile_pool(name="ring3", bufs=3))
        ring4 = ctx.enter_context(tc.tile_pool(name="ring4", bufs=4))
        psum = ctx.enter_context(tc.psum_pool(name="psum", bufs=8))
        ctx.enter_context(tc.manual_schedule())

        enc = {}
        w1_raw = {}
        w1_grouped = {}
        w1_codes = {}
        w1_scales = {}
        h0_relu = {}
        h0_turned = {}
        h0_grouped = {}
        h0_codes = {}
        h0_scales = {}
        bank1 = {}
        h1_rows = {}
        h1_grouped = {}
        h1_codes = {}
        h1_scales = {}
        bank2 = {}
        prob = {}
        prob_turned = {}
        mixed = {}

        def load_enc(g, b):
            enc[(g, b)] = keep.tile([P, 2, H], BF16, name="enc%d_%d" % (g, b), tag="enc%d_%d" % (g, b))
            r0 = g * GT + b * 2 * P
            nc.sync.dma_start(
                out=enc[(g, b)][:], in_=encodings[r0 : r0 + 2 * P, :].rearrange("(j p) k -> p j k", p=P)
            )

        def load_w1(s):
            w1_raw[s] = keep.tile([P, PACK, H], BF16, name="w1raw%d" % s, tag="w1raw%d" % s)
            nc.sync.dma_start(out=w1_raw[s][:], in_=W1[s].rearrange("(p j) c -> p j c", j=PACK))

        ident = keep.tile([P, P], F32, name="ident", tag="ident")
        make_identity(nc, ident[:])

        b1_bf = keep.tile([P, S, PACK], BF16, name="b1_bf", tag="b1_bf")
        nc.scalar.dma_start(out=b1_bf[:], in_=b1.rearrange("s (p t) -> p s t", t=PACK))
        b2_bf = keep.tile([P, S], BF16, name="b2_bf", tag="b2_bf")
        with nc.allow_non_contiguous_dma(reason="512 bias values, one to a partition, once"):
            nc.scalar.dma_start(out=b2_bf[:], in_=b2.rearrange("s t -> t s"))

        load_enc(0, 0)
        load_enc(0, 1)
        load_w1(0)
        load_w1(1)
        load_enc(1, 0)
        load_enc(1, 1)
        load_w1(2)
        w2_raw = keep.tile([P, S, PACK, T], BF16, name="w2_raw", tag="w2_raw")
        nc.sync.dma_start(out=w2_raw[:], in_=W2.rearrange("s (p j) c -> p s j c", j=PACK))
        load_w1(3)
        al_raw = keep.tile([P, P], BF16, name="al_raw", tag="al_raw")
        nc.sync.dma_start(out=al_raw[:], in_=alphas.rearrange("s (j p) -> (s j) p", p=P))
        for g in range(2, NG):
            load_enc(g, 0)
            load_enc(g, 1)

        def relu_enc(g, b):
            h0_relu[(g, b)] = ring4.tile([P, 2, H], BF16, name="h0_relu", tag="h0_relu")
            nc.vector.tensor_scalar(
                out=h0_relu[(g, b)][:].rearrange("p j k -> p (j k)"),
                in0=enc[(g, b)][:].rearrange("p j k -> p (j k)"),
                scalar1=0.0,
                scalar2=None,
                op0=MAX,
            )

        def turn_enc(g, b):
            xt = psum.tile([P, 2, 2, P], F32, name="xt", tag="bank")
            h0_turned[(g, b)] = xt
            for jj in range(2):
                words = h0_relu[(g, b)][:, jj, :].bitcast(F32)
                for u in range(2):
                    nc.tensor.transpose(xt[:, jj, u, :], words[:, u : H // 2 : 2], ident[:])

        def copy_enc(g, b, engine):
            if b == 0:
                h0_grouped[g] = ring2.tile([P, GT * PACK], BF16, name="h0_grouped", tag="h0_grouped", align_bytes=64)
            dst = h0_grouped[g][:, b * 1024 : (b + 1) * 1024].bitcast(F32).rearrange(
                "p (jj r u) -> p jj r u", jj=2, u=2
            )
            src = h0_turned[(g, b)][:].rearrange("p jj u r -> p jj r u")
            if engine == "scalar":
                nc.scalar.copy(out=dst, in_=src)
            else:
                nc.vector.tensor_copy(out=dst, in_=src)

        def quantize_enc(g):
            h0_codes[g] = ring2.tile([P, GT], U32, name="h0_codes", tag="h0_codes", align_bytes=64)
            h0_scales[g] = ring2.tile([P, GT], U8, name="h0_scales", tag="h0_scales", align_bytes=64)
            nc.vector.quantize_mx(out=h0_codes[g][:].bitcast(FP8X4), scales=h0_scales[g][:], in_=h0_grouped[g][:])

        def group_w1(s, t0, nt, engine):
            if t0 == 0:
                w1_grouped[s] = ring2.tile([P, H * PACK], BF16, name="w1_grouped", tag="w1_grouped", align_bytes=64)
            dst = w1_grouped[s][:, t0 * H : (t0 + nt) * H].rearrange("p (t m j) -> p t m j", t=nt, j=PACK)
            src = w1_raw[s][:].rearrange("p j (m t) -> p t m j", t=PACK)[:, t0 : t0 + nt]
            if engine == "scalar":
                nc.scalar.copy(out=dst, in_=src)
            else:
                nc.vector.tensor_copy(out=dst, in_=src)

        def quantize_w1(s, t0, nt):
            if t0 == 0:
                w1_codes[s] = keep.tile([P, H], U32, name="w1c%d" % s, tag="w1c%d" % s, align_bytes=64)
                w1_scales[s] = keep.tile([P, H], U8, name="w1s%d" % s, tag="w1s%d" % s, align_bytes=64)
            nc.vector.quantize_mx(
                out=w1_codes[s][:, t0 * P : (t0 + nt) * P].bitcast(FP8X4),
                scales=w1_scales[s][:, t0 * P : (t0 + nt) * P],
                in_=w1_grouped[s][:, t0 * H : (t0 + nt) * H],
            )

        def stage1(u):
            g, s = divmod(u, S)
            for t in range(PACK):
                bank = psum.tile([P, GT], BANK1, name="bank1", tag="bank")
                bank1[(u, t)] = bank
                cols = slice(t * P, (t + 1) * P)
                nc.tensor.matmul_mx(
                    out=bank[:],
                    lhsT=w1_codes[s][:, cols].bitcast(FP8X4),
                    lhsT_scale=w1_scales[s][:, cols],
                    rhs=h0_codes[g][:].bitcast(FP8X4),
                    rhs_scale=h0_scales[g][:],
                    start=True,
                    stop=True,
                )

        def vector_reads(k):
            u, n0, n = ITEMS[k]
            if u % S == S - 1 and u >= S and n0 == 0:
                return [PACK - 1]
            return []

        def read1_alloc(k):
            n = ITEMS[k][2]
            h1_rows[k] = ring3.tile([P, PACK, n], BF16, name="h1_rows", tag="h1_rows")

        def read1(k, t, engine):
            u, n0, n = ITEMS[k]
            s = u % S
            bias = b1_f[:, s * PACK + t : s * PACK + t + 1]
            if engine == "scalar":
                nc.scalar.activation(
                    out=h1_rows[k][:, t, :], in_=bank1[(u, t)][:, n0 : n0 + n], func=RELU, bias=bias, scale=1.0
                )
            else:
                nc.vector.tensor_scalar(
                    out=h1_rows[k][:, t, :],
                    in0=bank1[(u, t)][:, n0 : n0 + n],
                    scalar1=bias,
                    scalar2=0.0,
                    op0=ADD,
                    op1=MAX,
                )

        def group_h1(k):
            n = ITEMS[k][2]
            h1_grouped[k] = ring2.tile([P, n * PACK], BF16, name="h1_grouped", tag="h1_grouped", align_bytes=64)
            nc.vector.tensor_copy(
                out=h1_grouped[k][:].rearrange("p (c i t) -> p c t i", i=4, t=PACK),
                in_=h1_rows[k][:].rearrange("p t (c i) -> p c t i", i=4),
            )

        def quantize_h1(k):
            n = ITEMS[k][2]
            h1_codes[k] = ring4.tile([P, n], U32, name="h1_codes", tag="h1_codes", align_bytes=64)
            h1_scales[k] = ring4.tile([P, n], U8, name="h1_scales", tag="h1_scales", align_bytes=64)
            nc.vector.quantize_mx(out=h1_codes[k][:].bitcast(FP8X4), scales=h1_scales[k][:], in_=h1_grouped[k][:])

        def stage2(k):
            u, n0, n = ITEMS[k]
            s = u % S
            bank2[k] = psum.tile([P, n], F32, name="bank2", tag="bank")
            cols = slice(s * T, (s + 1) * T)
            nc.tensor.matmul_mx(
                out=bank2[k][:],
                lhsT=w2_codes[:, cols].bitcast(FP8X4),
                lhsT_scale=w2_scales[:, cols],
                rhs=h1_codes[k][:].bitcast(FP8X4),
                rhs_scale=h1_scales[k][:],
                start=True,
                stop=True,
            )

        def sigmoid2(k):
            u, n0, n = ITEMS[k]
            s = u % S
            prob[k] = ring3.tile([P, n], F32, name="prob", tag="prob")
            nc.scalar.activation(out=prob[k][:], in_=bank2[k][:], func=SIGMOID, bias=b2_f[:, s : s + 1], scale=1.0)

        def turn_prob(k):
            n = ITEMS[k][2]
            prob_turned[k] = psum.tile([P, n // P, T], F32, name="prob_turned", tag="bank")
            for j in range(n // P):
                nc.tensor.transpose(prob_turned[k][:, j, :], prob[k][:, j * P : (j + 1) * P], ident[:])

        def mix(k):
            u, n0, n = ITEMS[k]
            g, s = divmod(u, S)
            if s == 0:
                mixed[g] = ring2.tile([P, 4, T], F32, name="mixed", tag="mixed")
            for jj in range(n // P):
                j = n0 // P + jj
                col = s * (N_TOK // P) + g * 4 + j
                if s == 0:
                    nc.vector.tensor_scalar(
                        out=mixed[g][:, j, :],
                        in0=prob_turned[k][:, jj, :],
                        scalar1=al_f[:, col : col + 1],
                        scalar2=None,
                        op0=MULT,
                    )
                else:
                    nc.vector.scalar_tensor_tensor(
                        out=mixed[g][:, j, :],
                        in0=prob_turned[k][:, jj, :],
                        scalar=al_f[:, col : col + 1],
                        in1=mixed[g][:, j, :],
                        op0=MULT,
                        op1=ADD,
                    )

        def store(k):
            u, n0, n = ITEMS[k]
            g = u // S
            r0 = g * GT + n0
            nc.sync.dma_start(
                out=out[r0 : r0 + n, :].rearrange("(j p) t -> p j t", p=P),
                in_=mixed[g][:, n0 // P : (n0 + n) // P, :],
            )

        warm_in = keep.tile([P, 1], F32, name="warm_in", tag="warm_in")
        warm_out = keep.tile([P, 1], F32, name="warm_out", tag="warm_out")
        nc.vector.memset(warm_in[:], 0.0)
        nc.scalar.activation(out=warm_out[:], in_=warm_in[:], func=SIGMOID)

        b1_f = keep.tile([P, S * PACK], F32, name="b1_f", tag="b1_f")
        b2_f = keep.tile([P, S], F32, name="b2_f", tag="b2_f")
        al_cast = keep.tile([P, P], F32, name="al_cast", tag="al_cast")
        al_f = keep.tile([P, P], F32, name="al_f", tag="al_f")
        w2_grouped = keep.tile([P, S * T * PACK], BF16, name="w2_grouped", tag="w2_grouped", align_bytes=64)
        w2_codes = keep.tile([P, S * T], U32, name="w2_codes", tag="w2_codes", align_bytes=64)
        w2_scales = keep.tile([P, S * T], U8, name="w2_scales", tag="w2_scales", align_bytes=64)

        relu_enc(0, 0)
        turn_enc(0, 0)
        copy_enc(0, 0, "scalar")
        relu_enc(0, 1)
        turn_enc(0, 1)
        copy_enc(0, 1, "vector")
        group_w1(0, 0, 2, "vector")
        group_w1(0, 2, 2, "scalar")
        nc.vector.tensor_copy(out=b1_f[:], in_=b1_bf[:].rearrange("p s t -> p (s t)"))
        quantize_enc(0)
        quantize_w1(0, 0, 2)
        quantize_w1(0, 2, 2)
        group_w1(1, 0, 2, "vector")
        group_w1(1, 2, 2, "scalar")
        relu_enc(1, 0)

        for i in range(-1, NI + 5):
            if 0 <= i - 3 < NI:
                stage2(i - 3)
            if 0 <= i - 4 < NI:
                turn_prob(i - 4)
            if i == 1:
                al_turned = psum.tile([P, P], F32, name="al_turned", tag="bank")
                nc.tensor.transpose(al_turned[:], al_cast[:], ident[:])
            if (i + 4) % 4 == 0 and 1 <= (i + 4) // 4 < NG:
                turn_enc((i + 4) // 4, 0)
            if (i + 3) % 4 == 0 and 1 <= (i + 3) // 4 < NG:
                turn_enc((i + 3) // 4, 1)
            if 0 <= i + 1 < NU:
                stage1(i + 1)
            if 0 <= i < NI:
                read1_alloc(i)
                for t in range(PACK):
                    if t not in vector_reads(i):
                        read1(i, t, "scalar")
            if 0 <= i - 3 < NI:
                sigmoid2(i - 3)
            if (i + 4) % 4 == 0 and 1 <= (i + 4) // 4 < NG:
                copy_enc((i + 4) // 4, 0, "scalar")
            if (i + 3) % 4 == 0 and 1 <= (i + 3) // 4 <= LAST_GROUP_ALL_SCALAR:
                copy_enc((i + 3) // 4, 1, "scalar")
            if 0 <= i < NI:
                for t in vector_reads(i):
                    read1(i, t, "vector")
            if 0 <= i - 1 < NI:
                group_h1(i - 1)
            if (i + 5) % 4 == 0 and 2 <= (i + 5) // 4 < NG:
                relu_enc((i + 5) // 4, 0)
            if (i + 4) % 4 == 0 and 1 <= (i + 4) // 4 < NG:
                relu_enc((i + 4) // 4, 1)
            if i == -1:
                quantize_w1(1, 0, 4)
                group_w1(2, 0, 4, "vector")
                nc.vector.tensor_copy(
                    out=w2_grouped[:].rearrange("p (s c j) -> p s c j", s=S, j=PACK),
                    in_=w2_raw[:].rearrange("p s j c -> p s c j"),
                )
                quantize_w1(2, 0, 4)
            if i == 0:
                group_w1(3, 0, 4, "vector")
                nc.vector.quantize_mx(out=w2_codes[:].bitcast(FP8X4), scales=w2_scales[:], in_=w2_grouped[:])
                nc.vector.tensor_copy(out=b2_f[:], in_=b2_bf[:])
                nc.vector.tensor_copy(out=al_cast[:], in_=al_raw[:])
                quantize_w1(3, 0, 4)
            if i == 1:
                nc.vector.tensor_copy(out=al_f[:], in_=al_turned[:])
            if 0 <= i - 4 < NI:
                mix(i - 4)
            if 0 <= i - 1 < NI:
                quantize_h1(i - 1)
            if (i + 3) % 4 == 0 and LAST_GROUP_ALL_SCALAR < (i + 3) // 4 < NG:
                copy_enc((i + 3) // 4, 1, "vector")
            if (i + 2) % 4 == 0 and 1 <= (i + 2) // 4 < NG:
                quantize_enc((i + 2) // 4)
            if 0 <= i - 4 < NI and ITEMS[i - 4][0] % S == S - 1:
                store(i - 4)
